import numpy as np
import ml_dtypes

BF16 = ml_dtypes.bfloat16


def bf(x):
    return np.asarray(x, np.float32).astype(BF16)


def f32(x):
    return np.asarray(x, np.float32)


def f64(x):
    return np.asarray(x).astype(np.float64)


def striped(idx):
    return np.tile(idx.reshape(-1, 16).T, (8, 1))


V, D, N = 2048, 128, 512


def elu(v):
    return np.maximum(v, 0.0) + np.exp(np.minimum(v, 0.0)) - 1.0


def setup_inputs():
    return {
        "table": bf(np.random.uniform(-0.9, 0.9, (D, V))),
        "wh": bf(2.0 * np.random.standard_normal((D, D)) / np.sqrt(D)),
        "bh": f32(0.2 * np.random.standard_normal((D, 1))),
        "w1": bf(np.random.standard_normal((D, D)) / np.sqrt(D)),
        "w2": bf(np.random.standard_normal((D, D)) / np.sqrt(D)),
        "ba": f32(0.2 * np.random.standard_normal((D, 1))),
        "offs": striped(np.random.permutation(np.tile(np.arange(V), 2))[:N]),
    }


def reference(table, wh, bh, w1, w2, ba, offs):
    idx = offs[:16].T.reshape(-1)
    h = elu(f64(wh).T @ f64(table)[:, idx] + f64(bh))
    return np.concatenate([h, f64(w1).T @ h + f64(ba), f64(w2).T @ h], axis=0)

@@ -1,0 +1,57 @@
+import concourse.mybir as mybir
+
+D = 128
+V = 2048
+N = 512
+
+BF16, F32, U16 = mybir.dt.bfloat16, mybir.dt.float32, mybir.dt.uint16
+ACT = mybir.ActivationFunctionType
+ALU = mybir.AluOpType
+
+FLOPS = 3 * 2 * D * D * N
+
+
+def tile_disan_kernel(tc, table, wh, bh, w1, w2, ba, offs, out):
+    nc = tc.nc
+    with (
+        tc.tile_pool(name="held", bufs=1) as held,
+        tc.psum_pool(name="psum", bufs=1) as psum,
+    ):
+        offsets = held.tile([D, N // 16], U16, name="offsets")
+        nc.sync.dma_start(offsets[:], offs)
+        table_sb = held.tile([D, V], BF16, name="table_sb")
+        nc.sync.dma_start(table_sb[:], table)
+        wh_sb = held.tile([D, D], BF16, name="wh_sb")
+        nc.scalar.dma_start(wh_sb[:], wh)
+        bh_sb = held.tile([D, 1], F32, name="bh_sb")
+        nc.scalar.dma_start(bh_sb[:], bh)
+        w1_sb = held.tile([D, D], BF16, name="w1_sb")
+        nc.scalar.dma_start(w1_sb[:], w1)
+        w2_sb = held.tile([D, D], BF16, name="w2_sb")
+        nc.scalar.dma_start(w2_sb[:], w2)
+        ba_sb = held.tile([D, 1], F32, name="ba_sb")
+        nc.scalar.dma_start(ba_sb[:], ba)
+
+        v_ps = psum.tile([D, N], F32, name="v_ps")
+        nc.tensor.matmul(v_ps[:], wh_sb[:], table_sb[:].indirect(offsets[:]), start=True, stop=True)
+
+        exp_v = held.tile([D, N], F32, name="exp_v")
+        nc.scalar.activation(exp_v[:], v_ps[:], ACT.Exp, bias=bh_sb[:])
+        neg_part = held.tile([D, N], F32, name="neg_part")
+        nc.vector.tensor_scalar(neg_part[:], exp_v[:], -1.0, 0.0, ALU.add, ALU.min)
+        h_bf = held.tile([D, N], BF16, name="h_bf")
+        nc.vector.scalar_tensor_tensor(h_bf[:], v_ps[:], bh_sb[:], neg_part[:], ALU.add, ALU.max)
+        h = held.tile([D, N], F32, name="h")
+        nc.vector.scalar_tensor_tensor(h[:], v_ps[:], bh_sb[:], neg_part[:], ALU.add, ALU.max)
+        nc.sync.dma_start(out[0:D, :], h[:])
+
+        p_ps = psum.tile([D, N], F32, name="p_ps")
+        nc.tensor.matmul(p_ps[:], w1_sb[:], h_bf[:], start=True, stop=True)
+        q_ps = psum.tile([D, N], F32, name="q_ps")
+        nc.tensor.matmul(q_ps[:], w2_sb[:], h_bf[:], start=True, stop=True)
+        p = held.tile([D, N], F32, name="p")
+        nc.scalar.activation(p[:], p_ps[:], ACT.Identity, bias=ba_sb[:])
+        nc.scalar.dma_start(out[D : 2 * D, :], p[:])
+        q = held.tile([D, N], F32, name="q")
+        nc.vector.tensor_copy(q[:], q_ps[:])
+        nc.sync.dma_start(out[2 * D : 3 * D, :], q[:])

@@ -17,20 +17,24 @@ def tile_disan_kernel(tc, table, wh, bh, w1, w2, ba, offs, out):
         tc.tile_pool(name="held", bufs=1) as held,
         tc.psum_pool(name="psum", bufs=1) as psum,
     ):
+        table_sb = held.tile([D, V], BF16, name="table_sb")
+        nc.scalar.dma_start(table_sb[:], table)
         offsets = held.tile([D, N // 16], U16, name="offsets")
         nc.sync.dma_start(offsets[:], offs)
-        table_sb = held.tile([D, V], BF16, name="table_sb")
-        nc.sync.dma_start(table_sb[:], table)
         wh_sb = held.tile([D, D], BF16, name="wh_sb")
-        nc.scalar.dma_start(wh_sb[:], wh)
+        nc.sync.dma_start(wh_sb[:], wh)
         bh_sb = held.tile([D, 1], F32, name="bh_sb")
-        nc.scalar.dma_start(bh_sb[:], bh)
+        nc.sync.dma_start(bh_sb[:], bh)
         w1_sb = held.tile([D, D], BF16, name="w1_sb")
-        nc.scalar.dma_start(w1_sb[:], w1)
+        nc.gpsimd.dma_start(w1_sb[:], w1)
         w2_sb = held.tile([D, D], BF16, name="w2_sb")
-        nc.scalar.dma_start(w2_sb[:], w2)
+        nc.gpsimd.dma_start(w2_sb[:], w2)
         ba_sb = held.tile([D, 1], F32, name="ba_sb")
-        nc.scalar.dma_start(ba_sb[:], ba)
+        nc.gpsimd.dma_start(ba_sb[:], ba)
+
+        warm = held.tile([D, 1], F32, name="warm")
+        nc.vector.memset(warm[:], 0.0)
+        nc.scalar.activation(warm[:], warm[:], ACT.Exp)
 
         v_ps = psum.tile([D, N], F32, name="v_ps")
         nc.tensor.matmul(v_ps[:], wh_sb[:], table_sb[:].indirect(offsets[:]), start=True, stop=True)

@@ -10,6 +10,8 @@ ALU = mybir.AluOpType
 
 FLOPS = 3 * 2 * D * D * N
 
+TABLE_LOADS = 4
+
 
 def tile_disan_kernel(tc, table, wh, bh, w1, w2, ba, offs, out):
     nc = tc.nc
@@ -17,20 +19,23 @@ def tile_disan_kernel(tc, table, wh, bh, w1, w2, ba, offs, out):
         tc.tile_pool(name="held", bufs=1) as held,
         tc.psum_pool(name="psum", bufs=1) as psum,
     ):
-        table_sb = held.tile([D, V], BF16, name="table_sb")
-        nc.scalar.dma_start(table_sb[:], table)
         offsets = held.tile([D, N // 16], U16, name="offsets")
         nc.sync.dma_start(offsets[:], offs)
+        table_sb = held.tile([D, V], BF16, name="table_sb")
+        block = V // TABLE_LOADS
+        for b in range(TABLE_LOADS):
+            queue = nc.scalar if b % 2 == 0 else nc.sync
+            queue.dma_start(table_sb[:, b * block : (b + 1) * block], table[:, b * block : (b + 1) * block])
         wh_sb = held.tile([D, D], BF16, name="wh_sb")
-        nc.sync.dma_start(wh_sb[:], wh)
+        nc.scalar.dma_start(wh_sb[:], wh)
         bh_sb = held.tile([D, 1], F32, name="bh_sb")
         nc.sync.dma_start(bh_sb[:], bh)
         w1_sb = held.tile([D, D], BF16, name="w1_sb")
-        nc.gpsimd.dma_start(w1_sb[:], w1)
+        nc.scalar.dma_start(w1_sb[:], w1)
         w2_sb = held.tile([D, D], BF16, name="w2_sb")
-        nc.gpsimd.dma_start(w2_sb[:], w2)
+        nc.sync.dma_start(w2_sb[:], w2)
         ba_sb = held.tile([D, 1], F32, name="ba_sb")
-        nc.gpsimd.dma_start(ba_sb[:], ba)
+        nc.sync.dma_start(ba_sb[:], ba)
 
         warm = held.tile([D, 1], F32, name="warm")
         nc.vector.memset(warm[:], 0.0)

@@ -3,6 +3,8 @@ import concourse.mybir as mybir
 D = 128
 V = 2048
 N = 512
+PIECES = 4
+W = N // PIECES
 
 BF16, F32, U16 = mybir.dt.bfloat16, mybir.dt.float32, mybir.dt.uint16
 ACT = mybir.ActivationFunctionType
@@ -10,57 +12,60 @@ ALU = mybir.AluOpType
 
 FLOPS = 3 * 2 * D * D * N
 
-TABLE_LOADS = 4
-
 
 def tile_disan_kernel(tc, table, wh, bh, w1, w2, ba, offs, out):
     nc = tc.nc
     with (
         tc.tile_pool(name="held", bufs=1) as held,
-        tc.psum_pool(name="psum", bufs=1) as psum,
+        tc.psum_pool(name="psum_v", bufs=PIECES) as psum_v,
+        tc.psum_pool(name="psum_pq", bufs=2) as psum_pq,
     ):
+        table_sb = held.tile([D, V], BF16, name="table_sb")
+        nc.scalar.dma_start(table_sb[:], table)
         offsets = held.tile([D, N // 16], U16, name="offsets")
         nc.sync.dma_start(offsets[:], offs)
-        table_sb = held.tile([D, V], BF16, name="table_sb")
-        block = V // TABLE_LOADS
-        for b in range(TABLE_LOADS):
-            queue = nc.scalar if b % 2 == 0 else nc.sync
-            queue.dma_start(table_sb[:, b * block : (b + 1) * block], table[:, b * block : (b + 1) * block])
         wh_sb = held.tile([D, D], BF16, name="wh_sb")
-        nc.scalar.dma_start(wh_sb[:], wh)
+        nc.sync.dma_start(wh_sb[:], wh)
         bh_sb = held.tile([D, 1], F32, name="bh_sb")
         nc.sync.dma_start(bh_sb[:], bh)
         w1_sb = held.tile([D, D], BF16, name="w1_sb")
         nc.scalar.dma_start(w1_sb[:], w1)
         w2_sb = held.tile([D, D], BF16, name="w2_sb")
-        nc.sync.dma_start(w2_sb[:], w2)
+        nc.scalar.dma_start(w2_sb[:], w2)
         ba_sb = held.tile([D, 1], F32, name="ba_sb")
-        nc.sync.dma_start(ba_sb[:], ba)
+        nc.scalar.dma_start(ba_sb[:], ba)
 
         warm = held.tile([D, 1], F32, name="warm")
         nc.vector.memset(warm[:], 0.0)
         nc.scalar.activation(warm[:], warm[:], ACT.Exp)
 
-        v_ps = psum.tile([D, N], F32, name="v_ps")
-        nc.tensor.matmul(v_ps[:], wh_sb[:], table_sb[:].indirect(offsets[:]), start=True, stop=True)
-
         exp_v = held.tile([D, N], F32, name="exp_v")
-        nc.scalar.activation(exp_v[:], v_ps[:], ACT.Exp, bias=bh_sb[:])
-        neg_part = held.tile([D, N], F32, name="neg_part")
-        nc.vector.tensor_scalar(neg_part[:], exp_v[:], -1.0, 0.0, ALU.add, ALU.min)
-        h_bf = held.tile([D, N], BF16, name="h_bf")
-        nc.vector.scalar_tensor_tensor(h_bf[:], v_ps[:], bh_sb[:], neg_part[:], ALU.add, ALU.max)
+        relu_v = held.tile([D, N], F32, name="relu_v")
         h = held.tile([D, N], F32, name="h")
-        nc.vector.scalar_tensor_tensor(h[:], v_ps[:], bh_sb[:], neg_part[:], ALU.add, ALU.max)
-        nc.sync.dma_start(out[0:D, :], h[:])
+        h_bf = held.tile([D, N], BF16, name="h_bf")
+        pq = held.tile([D, 2, N], F32, name="pq")
+        out_pq = out[D : 3 * D, :].rearrange("(two d) n -> d two n", two=2)
+        pieces = [slice(c * W, (c + 1) * W) for c in range(PIECES)]
 
-        p_ps = psum.tile([D, N], F32, name="p_ps")
-        nc.tensor.matmul(p_ps[:], w1_sb[:], h_bf[:], start=True, stop=True)
-        q_ps = psum.tile([D, N], F32, name="q_ps")
-        nc.tensor.matmul(q_ps[:], w2_sb[:], h_bf[:], start=True, stop=True)
-        p = held.tile([D, N], F32, name="p")
-        nc.scalar.activation(p[:], p_ps[:], ACT.Identity, bias=ba_sb[:])
-        nc.scalar.dma_start(out[D : 2 * D, :], p[:])
-        q = held.tile([D, N], F32, name="q")
-        nc.vector.tensor_copy(q[:], q_ps[:])
-        nc.sync.dma_start(out[2 * D : 3 * D, :], q[:])
+        v_ps = [psum_v.tile([D, W], F32, name="v_ps") for _ in range(PIECES)]
+        for c in range(PIECES):
+            piece_offsets = offsets[:, c * (W // 16) : (c + 1) * (W // 16)]
+            nc.tensor.matmul(v_ps[c][:], wh_sb[:], table_sb[:].indirect(piece_offsets), start=True, stop=True)
+
+        for c, cols in enumerate(pieces):
+            nc.scalar.activation(exp_v[:, cols], v_ps[c][:], ACT.Exp, bias=bh_sb[:])
+            nc.scalar.activation(relu_v[:, cols], v_ps[c][:], ACT.Relu, bias=bh_sb[:])
+            nc.vector.scalar_tensor_tensor(h_bf[:, cols], exp_v[:, cols], -1.0, relu_v[:, cols], ALU.add, ALU.min)
+            nc.vector.scalar_tensor_tensor(h[:, cols], exp_v[:, cols], -1.0, relu_v[:, cols], ALU.add, ALU.min)
+            if c % 2 == 1:
+                pair = slice((c - 1) * W, (c + 1) * W)
+                nc.sync.dma_start(out[0:D, pair], h[:, pair])
+
+        for cols in pieces:
+            p_ps = psum_pq.tile([D, W], F32, name="p_ps")
+            nc.tensor.matmul(p_ps[:], w1_sb[:], h_bf[:, cols], start=True, stop=True)
+            q_ps = psum_pq.tile([D, W], F32, name="q_ps")
+            nc.tensor.matmul(q_ps[:], w2_sb[:], h_bf[:, cols], start=True, stop=True)
+            nc.scalar.activation(pq[:, 0, cols], p_ps[:], ACT.Identity, bias=ba_sb[:])
+            nc.vector.tensor_copy(pq[:, 1, cols], q_ps[:])
+            nc.sync.dma_start(out_pq[:, :, cols], pq[:, :, cols])

@@ -12,6 +12,8 @@ ALU = mybir.AluOpType
 
 FLOPS = 3 * 2 * D * D * N
 
+WARM_MATMULS = 4
+
 
 def tile_disan_kernel(tc, table, wh, bh, w1, w2, ba, offs, out):
     nc = tc.nc
@@ -38,6 +40,12 @@ def tile_disan_kernel(tc, table, wh, bh, w1, w2, ba, offs, out):
         warm = held.tile([D, 1], F32, name="warm")
         nc.vector.memset(warm[:], 0.0)
         nc.scalar.activation(warm[:], warm[:], ACT.Exp)
+
+        zeros = held.tile([D, N], BF16, name="zeros")
+        nc.gpsimd.memset(zeros[:], 0.0)
+        idle_ps = psum_pq.tile([D, N], F32, name="idle_ps", tag="p_ps")
+        for _ in range(WARM_MATMULS):
+            nc.tensor.matmul(idle_ps[:], zeros[:, 0:D], zeros[:], start=True, stop=True)
 
         exp_v = held.tile([D, N], F32, name="exp_v")
         relu_v = held.tile([D, N], F32, name="relu_v")

@@ -12,8 +12,6 @@ ALU = mybir.AluOpType
 
 FLOPS = 3 * 2 * D * D * N
 
-WARM_MATMULS = 4
-
 
 def tile_disan_kernel(tc, table, wh, bh, w1, w2, ba, offs, out):
     nc = tc.nc
@@ -31,21 +29,15 @@ def tile_disan_kernel(tc, table, wh, bh, w1, w2, ba, offs, out):
         bh_sb = held.tile([D, 1], F32, name="bh_sb")
         nc.sync.dma_start(bh_sb[:], bh)
         w1_sb = held.tile([D, D], BF16, name="w1_sb")
-        nc.scalar.dma_start(w1_sb[:], w1)
+        nc.sync.dma_start(w1_sb[:], w1)
         w2_sb = held.tile([D, D], BF16, name="w2_sb")
-        nc.scalar.dma_start(w2_sb[:], w2)
+        nc.sync.dma_start(w2_sb[:], w2)
         ba_sb = held.tile([D, 1], F32, name="ba_sb")
-        nc.scalar.dma_start(ba_sb[:], ba)
+        nc.sync.dma_start(ba_sb[:], ba)
 
         warm = held.tile([D, 1], F32, name="warm")
         nc.vector.memset(warm[:], 0.0)
         nc.scalar.activation(warm[:], warm[:], ACT.Exp)
-
-        zeros = held.tile([D, N], BF16, name="zeros")
-        nc.gpsimd.memset(zeros[:], 0.0)
-        idle_ps = psum_pq.tile([D, N], F32, name="idle_ps", tag="p_ps")
-        for _ in range(WARM_MATMULS):
-            nc.tensor.matmul(idle_ps[:], zeros[:, 0:D], zeros[:], start=True, stop=True)
 
         exp_v = held.tile([D, N], F32, name="exp_v")
         relu_v = held.tile([D, N], F32, name="relu_v")

@@ -29,11 +29,11 @@ def tile_disan_kernel(tc, table, wh, bh, w1, w2, ba, offs, out):
         bh_sb = held.tile([D, 1], F32, name="bh_sb")
         nc.sync.dma_start(bh_sb[:], bh)
         w1_sb = held.tile([D, D], BF16, name="w1_sb")
-        nc.sync.dma_start(w1_sb[:], w1)
+        nc.scalar.dma_start(w1_sb[:], w1)
         w2_sb = held.tile([D, D], BF16, name="w2_sb")
-        nc.sync.dma_start(w2_sb[:], w2)
+        nc.scalar.dma_start(w2_sb[:], w2)
         ba_sb = held.tile([D, 1], F32, name="ba_sb")
-        nc.sync.dma_start(ba_sb[:], ba)
+        nc.scalar.dma_start(ba_sb[:], ba)
 
         warm = held.tile([D, 1], F32, name="warm")
         nc.vector.memset(warm[:], 0.0)
@@ -57,15 +57,18 @@ def tile_disan_kernel(tc, table, wh, bh, w1, w2, ba, offs, out):
             nc.scalar.activation(relu_v[:, cols], v_ps[c][:], ACT.Relu, bias=bh_sb[:])
             nc.vector.scalar_tensor_tensor(h_bf[:, cols], exp_v[:, cols], -1.0, relu_v[:, cols], ALU.add, ALU.min)
             nc.vector.scalar_tensor_tensor(h[:, cols], exp_v[:, cols], -1.0, relu_v[:, cols], ALU.add, ALU.min)
-            if c % 2 == 1:
-                pair = slice((c - 1) * W, (c + 1) * W)
-                nc.sync.dma_start(out[0:D, pair], h[:, pair])
 
-        for cols in pieces:
+        for c, cols in enumerate(pieces):
             p_ps = psum_pq.tile([D, W], F32, name="p_ps")
             nc.tensor.matmul(p_ps[:], w1_sb[:], h_bf[:, cols], start=True, stop=True)
             q_ps = psum_pq.tile([D, W], F32, name="q_ps")
             nc.tensor.matmul(q_ps[:], w2_sb[:], h_bf[:, cols], start=True, stop=True)
             nc.scalar.activation(pq[:, 0, cols], p_ps[:], ACT.Identity, bias=ba_sb[:])
-            nc.vector.tensor_copy(pq[:, 1, cols], q_ps[:])
+            if c % 2 == 0:
+                nc.scalar.copy(pq[:, 1, cols], q_ps[:])
+            else:
+                nc.vector.tensor_copy(pq[:, 1, cols], q_ps[:])
+            if c < PIECES // 2:
+                pair = slice(2 * c * W, 2 * (c + 1) * W)
+                nc.sync.dma_start(out[0:D, pair], h[:, pair])
             nc.sync.dma_start(out_pq[:, :, cols], pq[:, :, cols])

@@ -4,6 +4,7 @@ D = 128
 V = 2048
 N = 512
 PIECES = 4
+BANKS = 8
 W = N // PIECES
 
 BF16, F32, U16 = mybir.dt.bfloat16, mybir.dt.float32, mybir.dt.uint16
@@ -17,8 +18,7 @@ def tile_disan_kernel(tc, table, wh, bh, w1, w2, ba, offs, out):
     nc = tc.nc
     with (
         tc.tile_pool(name="held", bufs=1) as held,
-        tc.psum_pool(name="psum_v", bufs=PIECES) as psum_v,
-        tc.psum_pool(name="psum_pq", bufs=2) as psum_pq,
+        tc.psum_pool(name="psum", bufs=BANKS) as psum,
     ):
         table_sb = held.tile([D, V], BF16, name="table_sb")
         nc.scalar.dma_start(table_sb[:], table)
@@ -47,7 +47,7 @@ def tile_disan_kernel(tc, table, wh, bh, w1, w2, ba, offs, out):
         out_pq = out[D : 3 * D, :].rearrange("(two d) n -> d two n", two=2)
         pieces = [slice(c * W, (c + 1) * W) for c in range(PIECES)]
 
-        v_ps = [psum_v.tile([D, W], F32, name="v_ps") for _ in range(PIECES)]
+        v_ps = [psum.tile([D, W], F32, name="v_ps", tag="bank") for _ in range(PIECES)]
         for c in range(PIECES):
             piece_offsets = offsets[:, c * (W // 16) : (c + 1) * (W // 16)]
             nc.tensor.matmul(v_ps[c][:], wh_sb[:], table_sb[:].indirect(piece_offsets), start=True, stop=True)
@@ -59,9 +59,9 @@ def tile_disan_kernel(tc, table, wh, bh, w1, w2, ba, offs, out):
             nc.vector.scalar_tensor_tensor(h[:, cols], exp_v[:, cols], -1.0, relu_v[:, cols], ALU.add, ALU.min)
 
         for c, cols in enumerate(pieces):
-            p_ps = psum_pq.tile([D, W], F32, name="p_ps")
+            p_ps = psum.tile([D, W], F32, name="p_ps", tag="bank")
             nc.tensor.matmul(p_ps[:], w1_sb[:], h_bf[:, cols], start=True, stop=True)
-            q_ps = psum_pq.tile([D, W], F32, name="q_ps")
+            q_ps = psum.tile([D, W], F32, name="q_ps", tag="bank")
             nc.tensor.matmul(q_ps[:], w2_sb[:], h_bf[:, cols], start=True, stop=True)
             nc.scalar.activation(pq[:, 0, cols], p_ps[:], ACT.Identity, bias=ba_sb[:])
             if c % 2 == 0:
@@ -71,4 +71,6 @@ def tile_disan_kernel(tc, table, wh, bh, w1, w2, ba, offs, out):
             if c < PIECES // 2:
                 pair = slice(2 * c * W, 2 * (c + 1) * W)
                 nc.sync.dma_start(out[0:D, pair], h[:, pair])
-            nc.sync.dma_start(out_pq[:, :, cols], pq[:, :, cols])
+            if c % 2 == 1:
+                pair = slice((c - 1) * W, (c + 1) * W)
+                nc.sync.dma_start(out_pq[:, :, pair], pq[:, :, pair])

@@ -27,7 +27,7 @@ def tile_disan_kernel(tc, table, wh, bh, w1, w2, ba, offs, out):
         wh_sb = held.tile([D, D], BF16, name="wh_sb")
         nc.sync.dma_start(wh_sb[:], wh)
         bh_sb = held.tile([D, 1], F32, name="bh_sb")
-        nc.sync.dma_start(bh_sb[:], bh)
+        nc.scalar.dma_start(bh_sb[:], bh)
         w1_sb = held.tile([D, D], BF16, name="w1_sb")
         nc.scalar.dma_start(w1_sb[:], w1)
         w2_sb = held.tile([D, D], BF16, name="w2_sb")

@@ -57,6 +57,7 @@ def tile_disan_kernel(tc, table, wh, bh, w1, w2, ba, offs, out):
             nc.scalar.activation(relu_v[:, cols], v_ps[c][:], ACT.Relu, bias=bh_sb[:])
             nc.vector.scalar_tensor_tensor(h_bf[:, cols], exp_v[:, cols], -1.0, relu_v[:, cols], ALU.add, ALU.min)
             nc.vector.scalar_tensor_tensor(h[:, cols], exp_v[:, cols], -1.0, relu_v[:, cols], ALU.add, ALU.min)
+            nc.sync.dma_start(out[0:D, cols], h[:, cols])
 
         for c, cols in enumerate(pieces):
             p_ps = psum.tile([D, W], F32, name="p_ps", tag="bank")
@@ -68,9 +69,6 @@ def tile_disan_kernel(tc, table, wh, bh, w1, w2, ba, offs, out):
                 nc.scalar.copy(pq[:, 1, cols], q_ps[:])
             else:
                 nc.vector.tensor_copy(pq[:, 1, cols], q_ps[:])
-            if c < PIECES // 2:
-                pair = slice(2 * c * W, 2 * (c + 1) * W)
-                nc.sync.dma_start(out[0:D, pair], h[:, pair])
             if c % 2 == 1:
                 pair = slice((c - 1) * W, (c + 1) * W)
                 nc.sync.dma_start(out_pq[:, :, pair], pq[:, :, pair])

@@ -43,8 +43,8 @@ def tile_disan_kernel(tc, table, wh, bh, w1, w2, ba, offs, out):
         relu_v = held.tile([D, N], F32, name="relu_v")
         h = held.tile([D, N], F32, name="h")
         h_bf = held.tile([D, N], BF16, name="h_bf")
-        pq = held.tile([D, 2, N], F32, name="pq")
-        out_pq = out[D : 3 * D, :].rearrange("(two d) n -> d two n", two=2)
+        p = held.tile([D, N], F32, name="p")
+        q = held.tile([D, N], F32, name="q")
         pieces = [slice(c * W, (c + 1) * W) for c in range(PIECES)]
 
         v_ps = [psum.tile([D, W], F32, name="v_ps", tag="bank") for _ in range(PIECES)]
@@ -64,11 +64,12 @@ def tile_disan_kernel(tc, table, wh, bh, w1, w2, ba, offs, out):
             nc.tensor.matmul(p_ps[:], w1_sb[:], h_bf[:, cols], start=True, stop=True)
             q_ps = psum.tile([D, W], F32, name="q_ps", tag="bank")
             nc.tensor.matmul(q_ps[:], w2_sb[:], h_bf[:, cols], start=True, stop=True)
-            nc.scalar.activation(pq[:, 0, cols], p_ps[:], ACT.Identity, bias=ba_sb[:])
+            nc.scalar.activation(p[:, cols], p_ps[:], ACT.Identity, bias=ba_sb[:])
             if c % 2 == 0:
-                nc.scalar.copy(pq[:, 1, cols], q_ps[:])
+                nc.scalar.copy(q[:, cols], q_ps[:])
             else:
-                nc.vector.tensor_copy(pq[:, 1, cols], q_ps[:])
+                nc.vector.tensor_copy(q[:, cols], q_ps[:])
             if c % 2 == 1:
                 pair = slice((c - 1) * W, (c + 1) * W)
-                nc.sync.dma_start(out_pq[:, :, pair], pq[:, :, pair])
+                nc.sync.dma_start(out[D : 2 * D, pair], p[:, pair])
+                nc.sync.dma_start(out[2 * D : 3 * D, pair], q[:, pair])

@@ -59,17 +59,16 @@ def tile_disan_kernel(tc, table, wh, bh, w1, w2, ba, offs, out):
             nc.vector.scalar_tensor_tensor(h[:, cols], exp_v[:, cols], -1.0, relu_v[:, cols], ALU.add, ALU.min)
             nc.sync.dma_start(out[0:D, cols], h[:, cols])
 
-        for c, cols in enumerate(pieces):
-            p_ps = psum.tile([D, W], F32, name="p_ps", tag="bank")
-            nc.tensor.matmul(p_ps[:], w1_sb[:], h_bf[:, cols], start=True, stop=True)
-            q_ps = psum.tile([D, W], F32, name="q_ps", tag="bank")
-            nc.tensor.matmul(q_ps[:], w2_sb[:], h_bf[:, cols], start=True, stop=True)
-            nc.scalar.activation(p[:, cols], p_ps[:], ACT.Identity, bias=ba_sb[:])
-            if c % 2 == 0:
-                nc.scalar.copy(q[:, cols], q_ps[:])
-            else:
+        for first in range(0, PIECES, 2):
+            pair = pieces[first : first + 2]
+            both = slice(first * W, (first + 2) * W)
+            for cols in pair:
+                p_ps = psum.tile([D, W], F32, name="p_ps", tag="bank")
+                nc.tensor.matmul(p_ps[:], w1_sb[:], h_bf[:, cols], start=True, stop=True)
+                nc.scalar.activation(p[:, cols], p_ps[:], ACT.Identity, bias=ba_sb[:])
+            nc.sync.dma_start(out[D : 2 * D, both], p[:, both])
+            for cols in pair:
+                q_ps = psum.tile([D, W], F32, name="q_ps", tag="bank")
+                nc.tensor.matmul(q_ps[:], w2_sb[:], h_bf[:, cols], start=True, stop=True)
                 nc.vector.tensor_copy(q[:, cols], q_ps[:])
-            if c % 2 == 1:
-                pair = slice((c - 1) * W, (c + 1) * W)
-                nc.sync.dma_start(out[D : 2 * D, pair], p[:, pair])
-                nc.sync.dma_start(out[2 * D : 3 * D, pair], q[:, pair])
+            nc.sync.dma_start(out[2 * D : 3 * D, both], q[:, both])

@@ -55,8 +55,12 @@ def tile_disan_kernel(tc, table, wh, bh, w1, w2, ba, offs, out):
         for c, cols in enumerate(pieces):
             nc.scalar.activation(exp_v[:, cols], v_ps[c][:], ACT.Exp, bias=bh_sb[:])
             nc.scalar.activation(relu_v[:, cols], v_ps[c][:], ACT.Relu, bias=bh_sb[:])
-            nc.vector.scalar_tensor_tensor(h_bf[:, cols], exp_v[:, cols], -1.0, relu_v[:, cols], ALU.add, ALU.min)
-            nc.vector.scalar_tensor_tensor(h[:, cols], exp_v[:, cols], -1.0, relu_v[:, cols], ALU.add, ALU.min)
+            if c < PIECES // 2:
+                nc.vector.scalar_tensor_tensor(h_bf[:, cols], exp_v[:, cols], -1.0, relu_v[:, cols], ALU.add, ALU.min)
+                nc.vector.scalar_tensor_tensor(h[:, cols], exp_v[:, cols], -1.0, relu_v[:, cols], ALU.add, ALU.min)
+            else:
+                nc.vector.scalar_tensor_tensor(h[:, cols], exp_v[:, cols], -1.0, relu_v[:, cols], ALU.add, ALU.min)
+                nc.vector.scalar_tensor_tensor(h_bf[:, cols], exp_v[:, cols], -1.0, relu_v[:, cols], ALU.add, ALU.min)
             nc.sync.dma_start(out[0:D, cols], h[:, cols])
 
         for first in range(0, PIECES, 2):

import concourse.mybir as mybir

D = 128
V = 2048
N = 512
PIECES = 4
BANKS = 8
W = N // PIECES

BF16, F32, U16 = mybir.dt.bfloat16, mybir.dt.float32, mybir.dt.uint16
ACT = mybir.ActivationFunctionType
ALU = mybir.AluOpType

FLOPS = 3 * 2 * D * D * N


def tile_disan_kernel(tc, table, wh, bh, w1, w2, ba, offs, out):
    nc = tc.nc
    with (
        tc.tile_pool(name="held", bufs=1) as held,
        tc.psum_pool(name="psum", bufs=BANKS) as psum,
    ):
        table_sb = held.tile([D, V], BF16, name="table_sb")
        nc.scalar.dma_start(table_sb[:], table)
        offsets = held.tile([D, N // 16], U16, name="offsets")
        nc.sync.dma_start(offsets[:], offs)
        wh_sb = held.tile([D, D], BF16, name="wh_sb")
        nc.sync.dma_start(wh_sb[:], wh)
        bh_sb = held.tile([D, 1], F32, name="bh_sb")
        nc.scalar.dma_start(bh_sb[:], bh)
        w1_sb = held.tile([D, D], BF16, name="w1_sb")
        nc.scalar.dma_start(w1_sb[:], w1)
        w2_sb = held.tile([D, D], BF16, name="w2_sb")
        nc.scalar.dma_start(w2_sb[:], w2)
        ba_sb = held.tile([D, 1], F32, name="ba_sb")
        nc.scalar.dma_start(ba_sb[:], ba)

        warm = held.tile([D, 1], F32, name="warm")
        nc.vector.memset(warm[:], 0.0)
        nc.scalar.activation(warm[:], warm[:], ACT.Exp)

        exp_v = held.tile([D, N], F32, name="exp_v")
        relu_v = held.tile([D, N], F32, name="relu_v")
        h = held.tile([D, N], F32, name="h")
        h_bf = held.tile([D, N], BF16, name="h_bf")
        p = held.tile([D, N], F32, name="p")
        q = held.tile([D, N], F32, name="q")
        pieces = [slice(c * W, (c + 1) * W) for c in range(PIECES)]

        v_ps = [psum.tile([D, W], F32, name="v_ps", tag="bank") for _ in range(PIECES)]
        for c in range(PIECES):
            piece_offsets = offsets[:, c * (W // 16) : (c + 1) * (W // 16)]
            nc.tensor.matmul(v_ps[c][:], wh_sb[:], table_sb[:].indirect(piece_offsets), start=True, stop=True)

        for c, cols in enumerate(pieces):
            nc.scalar.activation(exp_v[:, cols], v_ps[c][:], ACT.Exp, bias=bh_sb[:])
            nc.scalar.activation(relu_v[:, cols], v_ps[c][:], ACT.Relu, bias=bh_sb[:])
            if c < PIECES // 2:
                nc.vector.scalar_tensor_tensor(h_bf[:, cols], exp_v[:, cols], -1.0, relu_v[:, cols], ALU.add, ALU.min)
                nc.vector.scalar_tensor_tensor(h[:, cols], exp_v[:, cols], -1.0, relu_v[:, cols], ALU.add, ALU.min)
            else:
                nc.vector.scalar_tensor_tensor(h[:, cols], exp_v[:, cols], -1.0, relu_v[:, cols], ALU.add, ALU.min)
                nc.vector.scalar_tensor_tensor(h_bf[:, cols], exp_v[:, cols], -1.0, relu_v[:, cols], ALU.add, ALU.min)
            nc.sync.dma_start(out[0:D, cols], h[:, cols])

        for first in range(0, PIECES, 2):
            pair = pieces[first : first + 2]
            both = slice(first * W, (first + 2) * W)
            for cols in pair:
                p_ps = psum.tile([D, W], F32, name="p_ps", tag="bank")
                nc.tensor.matmul(p_ps[:], w1_sb[:], h_bf[:, cols], start=True, stop=True)
                nc.scalar.activation(p[:, cols], p_ps[:], ACT.Identity, bias=ba_sb[:])
            nc.sync.dma_start(out[D : 2 * D, both], p[:, both])
            for cols in pair:
                q_ps = psum.tile([D, W], F32, name="q_ps", tag="bank")
                nc.tensor.matmul(q_ps[:], w2_sb[:], h_bf[:, cols], start=True, stop=True)
                nc.vector.tensor_copy(q[:, cols], q_ps[:])
            nc.sync.dma_start(out[2 * D : 3 * D, both], q[:, both])
